import numpy as np
import ml_dtypes


BF16 = ml_dtypes.bfloat16


def bf(x):
    return np.asarray(x, np.float32).astype(BF16)


def f64(x):
    return np.asarray(x).astype(np.float64)


E2M1 = np.array([0.0, 0.5, 1.0, 1.5, 2.0, 3.0, 4.0, 6.0, -0.0, -0.5, -1.0, -1.5, -2.0, -3.0, -4.0, -6.0])


def pack_weight(w, fmt):
    k, n = w.shape
    w = f64(bf(w)).reshape(k // 32, 32, n)
    amax = np.abs(w).max(1)
    if fmt == "e4m3":
        byte = np.frexp(amax)[1] - 1 + 127 - 7
    else:
        mant, ex = np.frexp(amax / 6.0)
        byte = np.where(mant > 0.5, ex, ex - 1) + 127
    byte = np.clip(np.where(amax > 0, byte, 1), 1, 254)
    scaled = (w * np.exp2(127.0 - byte)[:, None, :]).reshape(k, n).astype(np.float32)
    by_word = np.ascontiguousarray(scaled.reshape(k // 512, 128, 4, n).transpose(0, 1, 3, 2))
    if fmt == "e4m3":
        words = by_word.astype(ml_dtypes.float8_e4m3fn).view(np.uint8)
    else:
        c = by_word.astype(ml_dtypes.float4_e2m1fn).view(np.uint8) & 0xF
        words = c[..., 0::2] | (c[..., 1::2] << 4)
    return np.ascontiguousarray(words), np.ascontiguousarray(byte.astype(np.uint8).reshape(k // 512, 16, n))


def unpack_weight(words, scales, fmt):
    g, p, n, _ = words.shape
    if fmt == "e4m3":
        vals = np.ascontiguousarray(words).view(ml_dtypes.float8_e4m3fn).astype(np.float64)
    else:
        nib = np.empty((g, p, n, 4), np.uint8)
        nib[..., 0::2] = words & 0xF
        nib[..., 1::2] = words >> 4
        vals = E2M1[nib]
    vals = vals * np.repeat(np.exp2(scales.astype(np.float64) - 127.0), 8, axis=1)[..., None]
    return vals.transpose(0, 1, 3, 2).reshape(g * 512, n)

def pack4(w):
    words, scales = pack_weight(w, "e2m1")
    return words.reshape(words.shape[0], 128, -1), scales


def unpack4(words, scales):
    return unpack_weight(words.reshape(words.shape[0], 128, -1, 2), scales, "e2m1")


def kspread(k):
    return np.exp2(np.repeat(np.random.randint(-6, 7, k // 32), 32).astype(np.float64))


B, S, E, H, DH, L = 2, 512, 2048, 16, 128, 512
NOPE = DH // 4
ROPE_D = DH - NOPE
THETA = 10000.0


def rope_tables(seq_len):
    freqs = 1.0 / THETA ** (np.arange(0, ROPE_D, 2) / ROPE_D)
    emb = np.arange(seq_len)[:, None] * freqs[None, :]
    return np.cos(emb), np.sin(emb)


def apply_rope(x, cos, sin):
    xe, xo = x[..., ::2], x[..., 1::2]
    return np.concatenate([xe * cos - xo * sin, xo * cos + xe * sin], axis=-1)


def setup_inputs():
    s = kspread(E)
    x = np.random.standard_normal((B, S, E)) * s
    x_words, x_scales = pack4(np.ascontiguousarray(x.reshape(B * S, E).T))
    words, scales = pack4(np.random.standard_normal((E, H * DH)) / np.sqrt(E) / s[:, None])
    return {"x_words": x_words, "x_scales": x_scales, "Wq_words": words, "Wq_scales": scales}


def reference(x_words, x_scales, Wq_words, Wq_scales):
    q = (unpack4(x_words, x_scales).T.reshape(B, S, E) @ unpack4(Wq_words, Wq_scales)).reshape(B, S, H, DH).transpose(0, 2, 1, 3)
    q_nope, q_rope = q[..., :NOPE], q[..., NOPE:]
    cos, sin = rope_tables(S)
    q_rope = apply_rope(q_rope, cos, sin)
    return np.concatenate([q_nope, q_rope], axis=-1)

@@ -1,0 +1,206 @@
+import math
+from contextlib import ExitStack
+
+import concourse.mybir as mybir
+
+F32 = mybir.dt.float32
+I32 = mybir.dt.int32
+U8 = mybir.dt.uint8
+FP4X4 = mybir.dt.float4_e2m1fn_x4
+ALU = mybir.AluOpType
+ACT = mybir.ActivationFunctionType
+
+P = 128
+PASSES = 4
+TOKENS = 1024
+HEADS = 16
+DH = 128
+NOPE = 32
+HALF = 48
+SEQ = 512
+N_TILE = 512
+HB = 4
+TOK_TILES = TOKENS // P
+POS_TILES = SEQ // P
+COL_BLOCKS = HEADS // HB
+
+FLOPS = 2 * TOKENS * 2048 * 2048
+
+
+def load_plane(nc, plane, scales):
+    for q in range(4):
+        nc.sync.dma_start(
+            out=plane[32 * q : 32 * q + 4, :, :].bitcast(I32),
+            in_=scales[:, 4 * q : 4 * q + 4, :].rearrange("g r n -> r g n").bitcast(I32),
+        )
+
+
+def load_codes(nc, codes, words):
+    nc.sync.dma_start(out=codes.bitcast(I32), in_=words.rearrange("g p n -> p g n").bitcast(I32))
+
+
+def tile_mla_pb_kernel(tc, x_words, x_scales, Wq_words, Wq_scales, out):
+    nc = tc.nc
+    with ExitStack() as ctx:
+        keep = ctx.enter_context(tc.tile_pool(name="keep", bufs=1))
+        work = ctx.enter_context(tc.tile_pool(name="work", bufs=6))
+        psum = ctx.enter_context(tc.psum_pool(name="psum", bufs=8))
+        ctx.enter_context(tc.manual_schedule())
+
+        xh = TOKENS // 2
+        xa_first = keep.tile([P, 1, 2 * xh], U8, name="xa_first", align_bytes=64)
+        xa_rest = keep.tile([P, PASSES - 1, 2 * xh], U8, name="xa_rest", align_bytes=64)
+        xb_codes = keep.tile([P, PASSES, 2 * xh], U8, name="xb_codes", align_bytes=64)
+        x_planes = [keep.tile([P, PASSES, xh], U8, name="x_plane%d" % c, align_bytes=64) for c in range(2)]
+        w0_first = keep.tile([P, 1, 2 * N_TILE], U8, name="w0_first", align_bytes=64)
+        w0_rest = keep.tile([P, PASSES - 1, 2 * N_TILE], U8, name="w0_rest", align_bytes=64)
+        w0_plane = keep.tile([P, PASSES, N_TILE], U8, name="w0_plane", align_bytes=64)
+        wr_codes = keep.tile([P, PASSES, 6 * N_TILE], U8, name="wr_codes", align_bytes=64)
+        wr_plane = keep.tile([P, PASSES, 3 * N_TILE], U8, name="wr_plane", align_bytes=64)
+
+        nc.vector.memset(w0_plane[:].bitcast(I32), 0)
+        nc.vector.memset(x_planes[0][:].bitcast(I32), 0)
+
+        pos = keep.tile([P, POS_TILES], F32, name="pos")
+        nc.gpsimd.iota(pos[:], pattern=[[P, POS_TILES]], base=0, channel_multiplier=1, allow_small_or_imprecise_dtypes=True)
+        nc.gpsimd.memset(x_planes[1][:].bitcast(F32), 0.0)
+        nc.gpsimd.memset(wr_plane[:].bitcast(F32), 0.0)
+
+        load_codes(nc, w0_first[:], Wq_words[0:1, :, 0 : 2 * N_TILE])
+        load_codes(nc, xa_first[:], x_words[0:1, :, 0 : 2 * xh])
+        load_plane(nc, w0_plane, Wq_scales[:, :, 0:N_TILE])
+        load_plane(nc, x_planes[0], x_scales[:, :, 0:xh])
+        load_codes(nc, w0_rest[:], Wq_words[1:PASSES, :, 0 : 2 * N_TILE])
+        load_codes(nc, xa_rest[:], x_words[1:PASSES, :, 0 : 2 * xh])
+        load_codes(nc, xb_codes[:], x_words[:, :, 2 * xh : 4 * xh])
+        load_plane(nc, x_planes[1], x_scales[:, :, xh : 2 * xh])
+        load_plane(nc, wr_plane, Wq_scales[:, :, N_TILE : 4 * N_TILE])
+        load_codes(nc, wr_codes[:], Wq_words[:, :, 2 * N_TILE : 8 * N_TILE])
+
+        def x_operand(i, g):
+            t0 = (i % 4) * P
+            if i >= 4:
+                codes = xb_codes[:, g, 2 * t0 : 2 * (t0 + P)]
+            elif g == 0:
+                codes = xa_first[:, 0, 2 * t0 : 2 * (t0 + P)]
+            else:
+                codes = xa_rest[:, g - 1, 2 * t0 : 2 * (t0 + P)]
+            return codes, x_planes[i // 4][:, g, t0 : t0 + P]
+
+        def w_operand(c0, n, g):
+            if c0 >= N_TILE:
+                c = c0 - N_TILE
+                return wr_codes[:, g, 2 * c : 2 * (c + n)], wr_plane[:, g, c : c + n]
+            if g == 0:
+                return w0_first[:, 0, 2 * c0 : 2 * (c0 + n)], w0_plane[:, g, c0 : c0 + n]
+            return w0_rest[:, g - 1, 2 * c0 : 2 * (c0 + n)], w0_plane[:, g, c0 : c0 + n]
+
+        ratio = 10000.0 ** (-1.0 / HALF)
+        theta = keep.tile([P, HALF], F32, name="theta")
+        nc.vector.memset(theta[:, 0:1], 1.0)
+        warm = keep.tile([P, 1], F32, name="warm")
+        nc.scalar.activation(out=warm[:], in_=theta[:, 0:1], func=ACT.Sin)
+        width = 1
+        while width < HALF:
+            n = min(width, HALF - width)
+            nc.vector.tensor_scalar(out=theta[:, width : width + n], in0=theta[:, 0:n], scalar1=ratio**width, scalar2=None, op0=ALU.mult)
+            width += n
+        turns = keep.tile([P, POS_TILES, HALF], F32, name="turns")
+        nc.vector.scalar_tensor_tensor(
+            out=turns[:],
+            in0=theta[:].unsqueeze(1).to_broadcast([P, POS_TILES, HALF]),
+            scalar=1.0 / (2.0 * math.pi),
+            in1=pos[:].unsqueeze(2).to_broadcast([P, POS_TILES, HALF]),
+            op0=ALU.mult,
+            op1=ALU.mult,
+        )
+        whole = keep.tile([P, POS_TILES, HALF], I32, name="whole")
+        nc.vector.tensor_copy(out=whole[:], in_=turns[:])
+        frac = keep.tile([P, POS_TILES, HALF], F32, name="frac")
+        nc.vector.tensor_tensor(out=frac[:], in0=turns[:], in1=whole[:], op=ALU.subtract)
+        shifted = keep.tile([P, POS_TILES, 4, HALF], F32, name="shifted")
+        frac2 = frac[:].unsqueeze(2).to_broadcast([P, POS_TILES, 2, HALF])
+        nc.vector.tensor_scalar(out=shifted[:, :, 0:4:3, :], in0=frac2, scalar1=0.25, scalar2=None, op0=ALU.add)
+        nc.vector.tensor_copy(out=shifted[:, :, 1:3, :], in_=frac2)
+        wrapped = keep.tile([P, POS_TILES, 4, HALF], F32, name="wrapped")
+        flat_s = shifted[:].rearrange("p a s j -> p (a s j)")
+        nc.vector.scalar_tensor_tensor(
+            out=wrapped[:].rearrange("p a s j -> p (a s j)"), in0=flat_s, scalar=0.5, in1=flat_s, op0=ALU.is_gt, op1=ALU.subtract
+        )
+        table = keep.tile([P, POS_TILES, 2, 2, HALF], F32, name="table")
+        tslots = table[:].rearrange("p a f e j -> p a (f e) j")
+        nc.scalar.activation(out=tslots[:, :, 0, :], in_=wrapped[:, :, 0, :], func=ACT.Sin, scale=-2.0 * math.pi)
+        nc.scalar.activation(out=tslots[:, :, 1, :], in_=wrapped[:, :, 1, :], func=ACT.Sin, scale=2.0 * math.pi)
+        nc.scalar.activation(out=tslots[:, :, 2:4, :], in_=wrapped[:, :, 2:4, :], func=ACT.Sin, scale=-2.0 * math.pi)
+
+        def multiply(pieces):
+            accs = [psum.tile([P, DH * nh], F32, name="acc", tag="acc") for (i, h0, nh) in pieces]
+            for g in range(PASSES):
+                for acc, (i, h0, nh) in zip(accs, pieces):
+                    lhsT, lhsT_scale = x_operand(i, g)
+                    rhs, rhs_scale = w_operand(DH * h0, DH * nh, g)
+                    nc.tensor.matmul_mx(
+                        out=acc[:],
+                        lhsT=lhsT.bitcast(FP4X4),
+                        lhsT_scale=lhsT_scale,
+                        rhs=rhs.bitcast(FP4X4),
+                        rhs_scale=rhs_scale,
+                        start=(g == 0),
+                        stop=(g == PASSES - 1),
+                    )
+            return accs
+
+        def products(acc, piece, prod, res, s0):
+            i, h0, nh = piece
+            heads = acc[:].rearrange("p (h d) -> p h d", h=nh)
+            pairs = heads[:, :, NOPE:DH].rearrange("p h (j e) -> p h e j", e=2)
+            for f in range(2):
+                nc.vector.tensor_tensor(
+                    out=prod[:, s0 : s0 + nh, f],
+                    in0=pairs,
+                    in1=table[:, i % POS_TILES, f].unsqueeze(1).to_broadcast([P, nh, 2, HALF]),
+                    op=ALU.mult,
+                )
+            nc.scalar.copy(out=res[:, s0 : s0 + nh, 0:NOPE], in_=heads[:, :, 0:NOPE])
+
+        def add_terms(engine, prod, res, ns):
+            rot = res[:, 0:ns, NOPE:DH].rearrange("p s (f j) -> p s f j", f=2)
+            engine.tensor_tensor(out=rot, in0=prod[:, 0:ns, :, 0, :], in1=prod[:, 0:ns, :, 1, :], op=ALU.add)
+
+        def store(piece, res, s0):
+            i, h0, nh = piece
+            p0 = (i % POS_TILES) * P
+            nc.sync.dma_start(
+                out=out[i // POS_TILES, h0 : h0 + nh, p0 : p0 + P, :].rearrange("h p d -> p h d"),
+                in_=res[:, s0 : s0 + nh, :],
+            )
+
+        def new_tiles():
+            prod = work.tile([P, 2 * HB, 2, 2, HALF], F32, name="prod", tag="prod")
+            res = work.tile([P, 2 * HB, DH], F32, name="res", tag="res")
+            return prod, res
+
+        banks = [(i, HB * nb, HB) for nb in range(COL_BLOCKS) for i in range(TOK_TILES)]
+        accs = {}
+        for piece, acc in zip(banks[0:4], multiply(banks[0:4])):
+            accs[piece] = acc
+        for k in range(0, 30, 2):
+            prod, res = new_tiles()
+            for u in range(2):
+                piece = banks[k + u]
+                if piece not in accs:
+                    accs[piece] = multiply([piece])[0]
+                products(accs[piece], piece, prod, res, HB * u)
+            add_terms(nc.gpsimd, prod, res, 2 * HB)
+            for u in range(2):
+                store(banks[k + u], res, HB * u)
+        tail = []
+        for (i, h0, nh), cuts in ((banks[30], ((0, 2), (2, 2))), (banks[31], ((0, 2),)), (banks[31], ((2, 1), (3, 1)))):
+            prod, res = new_tiles()
+            for s0, n in cuts:
+                piece = (i, h0 + s0, n)
+                products(multiply([piece])[0], piece, prod, res, s0 - cuts[0][0])
+            tail.append(((i, h0 + cuts[0][0], sum(n for s0, n in cuts)), prod, res))
+        for piece, prod, res in tail:
+            add_terms(nc.vector, prod, res, piece[2])
+            store(piece, res, 0)

@@ -5,6 +5,7 @@ import concourse.mybir as mybir
 
 F32 = mybir.dt.float32
 I32 = mybir.dt.int32
+BF16 = mybir.dt.bfloat16
 U8 = mybir.dt.uint8
 FP4X4 = mybir.dt.float4_e2m1fn_x4
 ALU = mybir.AluOpType
@@ -24,11 +25,13 @@ TOK_TILES = TOKENS // P
 POS_TILES = SEQ // P
 COL_BLOCKS = HEADS // HB
 
+WARM_UP = 12
+
 FLOPS = 2 * TOKENS * 2048 * 2048
 
 
 def load_plane(nc, plane, scales):
-    for q in range(4):
+    for q in (0, 2, 1, 3):
         nc.sync.dma_start(
             out=plane[32 * q : 32 * q + 4, :, :].bitcast(I32),
             in_=scales[:, 4 * q : 4 * q + 4, :].rearrange("g r n -> r g n").bitcast(I32),
@@ -43,7 +46,7 @@ def tile_mla_pb_kernel(tc, x_words, x_scales, Wq_words, Wq_scales, out):
     nc = tc.nc
     with ExitStack() as ctx:
         keep = ctx.enter_context(tc.tile_pool(name="keep", bufs=1))
-        work = ctx.enter_context(tc.tile_pool(name="work", bufs=6))
+        work = ctx.enter_context(tc.tile_pool(name="work", bufs=8))
         psum = ctx.enter_context(tc.psum_pool(name="psum", bufs=8))
         ctx.enter_context(tc.manual_schedule())
 
@@ -57,6 +60,12 @@ def tile_mla_pb_kernel(tc, x_words, x_scales, Wq_words, Wq_scales, out):
         w0_plane = keep.tile([P, PASSES, N_TILE], U8, name="w0_plane", align_bytes=64)
         wr_codes = keep.tile([P, PASSES, 6 * N_TILE], U8, name="wr_codes", align_bytes=64)
         wr_plane = keep.tile([P, PASSES, 3 * N_TILE], U8, name="wr_plane", align_bytes=64)
+
+        zeros = keep.tile([P, N_TILE], BF16, name="zeros")
+        nc.gpsimd.memset(zeros[:], 0.0)
+        idle = psum.tile([P, N_TILE], F32, name="acc", tag="acc")
+        for k in range(WARM_UP):
+            nc.tensor.matmul(out=idle[:], lhsT=zeros[:, 0:P], rhs=zeros[:], start=True, stop=True)
 
         nc.vector.memset(w0_plane[:].bitcast(I32), 0)
         nc.vector.memset(x_planes[0][:].bitcast(I32), 0)
@@ -165,7 +174,11 @@ def tile_mla_pb_kernel(tc, x_words, x_scales, Wq_words, Wq_scales, out):
 
         def add_terms(engine, prod, res, ns):
             rot = res[:, 0:ns, NOPE:DH].rearrange("p s (f j) -> p s f j", f=2)
-            engine.tensor_tensor(out=rot, in0=prod[:, 0:ns, :, 0, :], in1=prod[:, 0:ns, :, 1, :], op=ALU.add)
+            if engine is nc.vector:
+                for f in range(2):
+                    engine.tensor_tensor(out=rot[:, :, f, :], in0=prod[:, 0:ns, f, 0, :], in1=prod[:, 0:ns, f, 1, :], op=ALU.add)
+            else:
+                engine.tensor_tensor(out=rot, in0=prod[:, 0:ns, :, 0, :], in1=prod[:, 0:ns, :, 1, :], op=ALU.add)
 
         def store(piece, res, s0):
             i, h0, nh = piece
@@ -176,31 +189,37 @@ def tile_mla_pb_kernel(tc, x_words, x_scales, Wq_words, Wq_scales, out):
             )
 
         def new_tiles():
-            prod = work.tile([P, 2 * HB, 2, 2, HALF], F32, name="prod", tag="prod")
-            res = work.tile([P, 2 * HB, DH], F32, name="res", tag="res")
+            prod = work.tile([P, HB, 2, 2, HALF], F32, name="prod", tag="prod")
+            res = work.tile([P, HB, DH], F32, name="res", tag="res")
             return prod, res
 
         banks = [(i, HB * nb, HB) for nb in range(COL_BLOCKS) for i in range(TOK_TILES)]
         accs = {}
         for piece, acc in zip(banks[0:4], multiply(banks[0:4])):
             accs[piece] = acc
-        for k in range(0, 30, 2):
+        for k in range(30):
             prod, res = new_tiles()
-            for u in range(2):
-                piece = banks[k + u]
-                if piece not in accs:
-                    accs[piece] = multiply([piece])[0]
-                products(accs[piece], piece, prod, res, HB * u)
-            add_terms(nc.gpsimd, prod, res, 2 * HB)
-            for u in range(2):
-                store(banks[k + u], res, HB * u)
-        tail = []
-        for (i, h0, nh), cuts in ((banks[30], ((0, 2), (2, 2))), (banks[31], ((0, 2),)), (banks[31], ((2, 1), (3, 1)))):
+            piece = banks[k]
+            if piece not in accs:
+                accs[piece] = multiply([piece])[0]
+            products(accs[piece], piece, prod, res, 0)
+            add_terms(nc.vector if k % 4 == 3 else nc.gpsimd, prod, res, HB)
+            store(piece, res, 0)
+        def small_groups(bank, cuts):
+            i, h0, nh = bank
             prod, res = new_tiles()
             for s0, n in cuts:
                 piece = (i, h0 + s0, n)
                 products(multiply([piece])[0], piece, prod, res, s0 - cuts[0][0])
-            tail.append(((i, h0 + cuts[0][0], sum(n for s0, n in cuts)), prod, res))
-        for piece, prod, res in tail:
+            return (i, h0 + cuts[0][0], sum(n for s0, n in cuts)), prod, res
+
+        def finish(piece, prod, res):
             add_terms(nc.vector, prod, res, piece[2])
             store(piece, res, 0)
+
+        t30 = small_groups(banks[30], ((0, 2), (2, 2)))
+        t31a = small_groups(banks[31], ((0, 2),))
+        finish(*t30)
+        t31b = small_groups(banks[31], ((2, 1), (3, 1)))
+        finish(*t31a)
+        finish(*t31b)

@@ -189,22 +189,29 @@ def tile_mla_pb_kernel(tc, x_words, x_scales, Wq_words, Wq_scales, out):
             )
 
         def new_tiles():
-            prod = work.tile([P, HB, 2, 2, HALF], F32, name="prod", tag="prod")
-            res = work.tile([P, HB, DH], F32, name="res", tag="res")
+            prod = work.tile([P, 2 * HB, 2, 2, HALF], F32, name="prod", tag="prod")
+            res = work.tile([P, 2 * HB, DH], F32, name="res", tag="res")
             return prod, res
 
         banks = [(i, HB * nb, HB) for nb in range(COL_BLOCKS) for i in range(TOK_TILES)]
         accs = {}
         for piece, acc in zip(banks[0:4], multiply(banks[0:4])):
             accs[piece] = acc
-        for k in range(30):
+        for k in range(0, 26, 2):
             prod, res = new_tiles()
-            piece = banks[k]
-            if piece not in accs:
-                accs[piece] = multiply([piece])[0]
-            products(accs[piece], piece, prod, res, 0)
-            add_terms(nc.vector if k % 4 == 3 else nc.gpsimd, prod, res, HB)
-            store(piece, res, 0)
+            for u in range(2):
+                piece = banks[k + u]
+                if piece not in accs:
+                    accs[piece] = multiply([piece])[0]
+                products(accs[piece], piece, prod, res, HB * u)
+            add_terms(nc.gpsimd, prod, res, 2 * HB)
+            for u in range(2):
+                store(banks[k + u], res, HB * u)
+        for k in range(26, 30):
+            prod, res = new_tiles()
+            products(multiply([banks[k]])[0], banks[k], prod, res, 0)
+            add_terms(nc.gpsimd, prod, res, HB)
+            store(banks[k], res, 0)
         def small_groups(bank, cuts):
             i, h0, nh = bank
             prod, res = new_tiles()

@@ -136,49 +136,50 @@ def tile_mla_pb_kernel(tc, x_words, x_scales, Wq_words, Wq_scales, out):
         nc.vector.scalar_tensor_tensor(
             out=wrapped[:].rearrange("p a s j -> p (a s j)"), in0=flat_s, scalar=0.5, in1=flat_s, op0=ALU.is_gt, op1=ALU.subtract
         )
-        table = keep.tile([P, POS_TILES, 2, 2, HALF], F32, name="table")
-        tslots = table[:].rearrange("p a f e j -> p a (f e) j")
-        nc.scalar.activation(out=tslots[:, :, 0, :], in_=wrapped[:, :, 0, :], func=ACT.Sin, scale=-2.0 * math.pi)
-        nc.scalar.activation(out=tslots[:, :, 1, :], in_=wrapped[:, :, 1, :], func=ACT.Sin, scale=2.0 * math.pi)
-        nc.scalar.activation(out=tslots[:, :, 2:4, :], in_=wrapped[:, :, 2:4, :], func=ACT.Sin, scale=-2.0 * math.pi)
+        table = keep.tile([P, POS_TILES, 2, 2 * HALF], F32, name="table")
+        tslots = table[:].rearrange("p a f (j e) -> p a f e j", e=2)
+        nc.scalar.activation(out=tslots[:, :, 0, 0, :], in_=wrapped[:, :, 0, :], func=ACT.Sin, scale=-2.0 * math.pi)
+        nc.scalar.activation(out=tslots[:, :, 0, 1, :], in_=wrapped[:, :, 1, :], func=ACT.Sin, scale=2.0 * math.pi)
+        nc.scalar.activation(out=tslots[:, :, 1, :, :], in_=wrapped[:, :, 2:4, :], func=ACT.Sin, scale=-2.0 * math.pi)
+
+        def one_pass(acc, piece, g):
+            i, h0, nh = piece
+            lhsT, lhsT_scale = x_operand(i, g)
+            rhs, rhs_scale = w_operand(DH * h0, DH * nh, g)
+            nc.tensor.matmul_mx(
+                out=acc[:],
+                lhsT=lhsT.bitcast(FP4X4),
+                lhsT_scale=lhsT_scale,
+                rhs=rhs.bitcast(FP4X4),
+                rhs_scale=rhs_scale,
+                start=(g == 0),
+                stop=(g == PASSES - 1),
+            )
 
         def multiply(pieces):
             accs = [psum.tile([P, DH * nh], F32, name="acc", tag="acc") for (i, h0, nh) in pieces]
-            for g in range(PASSES):
-                for acc, (i, h0, nh) in zip(accs, pieces):
-                    lhsT, lhsT_scale = x_operand(i, g)
-                    rhs, rhs_scale = w_operand(DH * h0, DH * nh, g)
-                    nc.tensor.matmul_mx(
-                        out=acc[:],
-                        lhsT=lhsT.bitcast(FP4X4),
-                        lhsT_scale=lhsT_scale,
-                        rhs=rhs.bitcast(FP4X4),
-                        rhs_scale=rhs_scale,
-                        start=(g == 0),
-                        stop=(g == PASSES - 1),
-                    )
+            for acc, piece in zip(accs, pieces):
+                one_pass(acc, piece, 0)
+            for acc, piece in zip(accs, pieces):
+                for g in range(1, PASSES):
+                    one_pass(acc, piece, g)
             return accs
 
         def products(acc, piece, prod, res, s0):
             i, h0, nh = piece
             heads = acc[:].rearrange("p (h d) -> p h d", h=nh)
-            pairs = heads[:, :, NOPE:DH].rearrange("p h (j e) -> p h e j", e=2)
-            for f in range(2):
-                nc.vector.tensor_tensor(
-                    out=prod[:, s0 : s0 + nh, f],
-                    in0=pairs,
-                    in1=table[:, i % POS_TILES, f].unsqueeze(1).to_broadcast([P, nh, 2, HALF]),
-                    op=ALU.mult,
-                )
+            nc.vector.tensor_tensor(
+                out=prod[:, s0 : s0 + nh],
+                in0=heads[:, :, NOPE:DH].unsqueeze(2).to_broadcast([P, nh, 2, 2 * HALF]),
+                in1=table[:, i % POS_TILES].unsqueeze(1).to_broadcast([P, nh, 2, 2 * HALF]),
+                op=ALU.mult,
+            )
             nc.scalar.copy(out=res[:, s0 : s0 + nh, 0:NOPE], in_=heads[:, :, 0:NOPE])
 
         def add_terms(engine, prod, res, ns):
             rot = res[:, 0:ns, NOPE:DH].rearrange("p s (f j) -> p s f j", f=2)
-            if engine is nc.vector:
-                for f in range(2):
-                    engine.tensor_tensor(out=rot[:, :, f, :], in0=prod[:, 0:ns, f, 0, :], in1=prod[:, 0:ns, f, 1, :], op=ALU.add)
-            else:
-                engine.tensor_tensor(out=rot, in0=prod[:, 0:ns, :, 0, :], in1=prod[:, 0:ns, :, 1, :], op=ALU.add)
+            terms = prod[:, 0:ns].rearrange("p s f (j e) -> p s f e j", e=2)
+            engine.tensor_tensor(out=rot, in0=terms[:, :, :, 0, :], in1=terms[:, :, :, 1, :], op=ALU.add)
 
         def store(piece, res, s0):
             i, h0, nh = piece
@@ -189,7 +190,7 @@ def tile_mla_pb_kernel(tc, x_words, x_scales, Wq_words, Wq_scales, out):
             )
 
         def new_tiles():
-            prod = work.tile([P, 2 * HB, 2, 2, HALF], F32, name="prod", tag="prod")
+            prod = work.tile([P, 2 * HB, 2, 2 * HALF], F32, name="prod", tag="prod")
             res = work.tile([P, 2 * HB, DH], F32, name="res", tag="res")
             return prod, res
 

@@ -67,13 +67,11 @@ def tile_mla_pb_kernel(tc, x_words, x_scales, Wq_words, Wq_scales, out):
         for k in range(WARM_UP):
             nc.tensor.matmul(out=idle[:], lhsT=zeros[:, 0:P], rhs=zeros[:], start=True, stop=True)
 
-        nc.vector.memset(w0_plane[:].bitcast(I32), 0)
-        nc.vector.memset(x_planes[0][:].bitcast(I32), 0)
+        for plane in (w0_plane, x_planes[0], x_planes[1], wr_plane):
+            nc.vector.memset(plane[:].bitcast(I32), 0)
 
         pos = keep.tile([P, POS_TILES], F32, name="pos")
         nc.gpsimd.iota(pos[:], pattern=[[P, POS_TILES]], base=0, channel_multiplier=1, allow_small_or_imprecise_dtypes=True)
-        nc.gpsimd.memset(x_planes[1][:].bitcast(F32), 0.0)
-        nc.gpsimd.memset(wr_plane[:].bitcast(F32), 0.0)
 
         load_codes(nc, w0_first[:], Wq_words[0:1, :, 0 : 2 * N_TILE])
         load_codes(nc, xa_first[:], x_words[0:1, :, 0 : 2 * xh])

@@ -179,10 +179,10 @@ def tile_mla_pb_kernel(tc, x_words, x_scales, Wq_words, Wq_scales, out):
             terms = prod[:, 0:ns].rearrange("p s f (j e) -> p s f e j", e=2)
             engine.tensor_tensor(out=rot, in0=terms[:, :, :, 0, :], in1=terms[:, :, :, 1, :], op=ALU.add)
 
-        def store(piece, res, s0):
+        def store(piece, res, s0, queue=None):
             i, h0, nh = piece
             p0 = (i % POS_TILES) * P
-            nc.sync.dma_start(
+            (queue or nc.sync).dma_start(
                 out=out[i // POS_TILES, h0 : h0 + nh, p0 : p0 + P, :].rearrange("h p d -> p h d"),
                 in_=res[:, s0 : s0 + nh, :],
             )
@@ -219,13 +219,13 @@ def tile_mla_pb_kernel(tc, x_words, x_scales, Wq_words, Wq_scales, out):
                 products(multiply([piece])[0], piece, prod, res, s0 - cuts[0][0])
             return (i, h0 + cuts[0][0], sum(n for s0, n in cuts)), prod, res
 
-        def finish(piece, prod, res):
+        def finish(queue, piece, prod, res):
             add_terms(nc.vector, prod, res, piece[2])
-            store(piece, res, 0)
+            store(piece, res, 0, queue)
 
         t30 = small_groups(banks[30], ((0, 2), (2, 2)))
         t31a = small_groups(banks[31], ((0, 2),))
-        finish(*t30)
+        finish(nc.sync, *t30)
         t31b = small_groups(banks[31], ((2, 1), (3, 1)))
-        finish(*t31a)
-        finish(*t31b)
+        finish(nc.scalar, *t31a)
+        finish(nc.scalar, *t31b)

@@ -226,6 +226,8 @@ def tile_mla_pb_kernel(tc, x_words, x_scales, Wq_words, Wq_scales, out):
         t30 = small_groups(banks[30], ((0, 2), (2, 2)))
         t31a = small_groups(banks[31], ((0, 2),))
         finish(nc.sync, *t30)
-        t31b = small_groups(banks[31], ((2, 1), (3, 1)))
+        t31b = small_groups(banks[31], ((2, 1),))
+        t31c = small_groups(banks[31], ((3, 1),))
         finish(nc.scalar, *t31a)
-        finish(nc.scalar, *t31b)
+        finish(nc.sync, *t31b)
+        finish(nc.scalar, *t31c)

@@ -193,6 +193,7 @@ def tile_mla_pb_kernel(tc, x_words, x_scales, Wq_words, Wq_scales, out):
             return prod, res
 
         banks = [(i, HB * nb, HB) for nb in range(COL_BLOCKS) for i in range(TOK_TILES)]
+        queues = (nc.sync, nc.scalar)
         accs = {}
         for piece, acc in zip(banks[0:4], multiply(banks[0:4])):
             accs[piece] = acc
@@ -205,12 +206,12 @@ def tile_mla_pb_kernel(tc, x_words, x_scales, Wq_words, Wq_scales, out):
                 products(accs[piece], piece, prod, res, HB * u)
             add_terms(nc.gpsimd, prod, res, 2 * HB)
             for u in range(2):
-                store(banks[k + u], res, HB * u)
+                store(banks[k + u], res, HB * u, queues[u])
         for k in range(26, 30):
             prod, res = new_tiles()
             products(multiply([banks[k]])[0], banks[k], prod, res, 0)
             add_terms(nc.gpsimd, prod, res, HB)
-            store(banks[k], res, 0)
+            store(banks[k], res, 0, queues[(k + 1) % 2])
         def small_groups(bank, cuts):
             i, h0, nh = bank
             prod, res = new_tiles()
@@ -225,9 +226,9 @@ def tile_mla_pb_kernel(tc, x_words, x_scales, Wq_words, Wq_scales, out):
 
         t30 = small_groups(banks[30], ((0, 2), (2, 2)))
         t31a = small_groups(banks[31], ((0, 2),))
-        finish(nc.sync, *t30)
+        finish(nc.scalar, *t30)
         t31b = small_groups(banks[31], ((2, 1),))
         t31c = small_groups(banks[31], ((3, 1),))
-        finish(nc.scalar, *t31a)
-        finish(nc.sync, *t31b)
-        finish(nc.scalar, *t31c)
+        finish(nc.sync, *t31a)
+        finish(nc.scalar, *t31b)
+        finish(nc.sync, *t31c)

@@ -189,7 +189,7 @@ def tile_mla_pb_kernel(tc, x_words, x_scales, Wq_words, Wq_scales, out):
 
         def new_tiles():
             prod = work.tile([P, 2 * HB, 2, 2 * HALF], F32, name="prod", tag="prod")
-            res = work.tile([P, 2 * HB, DH], F32, name="res", tag="res")
+            res = work.tile([P, 2 * HB, DH], F32, name="res", tag="res", align_bytes=512)
             return prod, res
 
         banks = [(i, HB * nb, HB) for nb in range(COL_BLOCKS) for i in range(TOK_TILES)]

@@ -187,6 +187,12 @@ def tile_mla_pb_kernel(tc, x_words, x_scales, Wq_words, Wq_scales, out):
                 in_=res[:, s0 : s0 + nh, :],
             )
 
+        def store_halves(piece, res):
+            i, h0, nh = piece
+            half = nh // 2
+            store((i, h0, half), res, 0, nc.sync)
+            store((i, h0 + half, nh - half), res, half, nc.scalar)
+
         def new_tiles():
             prod = work.tile([P, 2 * HB, 2, 2 * HALF], F32, name="prod", tag="prod")
             res = work.tile([P, 2 * HB, DH], F32, name="res", tag="res", align_bytes=512)
@@ -211,7 +217,7 @@ def tile_mla_pb_kernel(tc, x_words, x_scales, Wq_words, Wq_scales, out):
             prod, res = new_tiles()
             products(multiply([banks[k]])[0], banks[k], prod, res, 0)
             add_terms(nc.gpsimd, prod, res, HB)
-            store(banks[k], res, 0, queues[(k + 1) % 2])
+            store_halves(banks[k], res)
         def small_groups(bank, cuts):
             i, h0, nh = bank
             prod, res = new_tiles()
@@ -222,7 +228,10 @@ def tile_mla_pb_kernel(tc, x_words, x_scales, Wq_words, Wq_scales, out):
 
         def finish(queue, piece, prod, res):
             add_terms(nc.vector, prod, res, piece[2])
-            store(piece, res, 0, queue)
+            if piece[2] > 1:
+                store_halves(piece, res)
+            else:
+                store(piece, res, 0, queue)
 
         t30 = small_groups(banks[30], ((0, 2), (2, 2)))
         t31a = small_groups(banks[31], ((0, 2),))

@@ -213,9 +213,14 @@ def tile_mla_pb_kernel(tc, x_words, x_scales, Wq_words, Wq_scales, out):
             add_terms(nc.gpsimd, prod, res, 2 * HB)
             for u in range(2):
                 store(banks[k + u], res, HB * u, queues[u])
-        for k in range(26, 30):
+        prod26, res26 = new_tiles()
+        products(multiply([banks[26]])[0], banks[26], prod26, res26, 0)
+        for k in range(27, 30):
             prod, res = new_tiles()
             products(multiply([banks[k]])[0], banks[k], prod, res, 0)
+            if k == 27:
+                add_terms(nc.vector, prod26, res26, HB)
+                store_halves(banks[26], res26)
             add_terms(nc.gpsimd, prod, res, HB)
             store_halves(banks[k], res)
         def small_groups(bank, cuts):

@@ -30,8 +30,8 @@ WARM_UP = 12
 FLOPS = 2 * TOKENS * 2048 * 2048
 
 
-def load_plane(nc, plane, scales):
-    for q in (0, 2, 1, 3):
+def load_plane(nc, plane, scales, quadrants=(0, 2, 1, 3)):
+    for q in quadrants:
         nc.sync.dma_start(
             out=plane[32 * q : 32 * q + 4, :, :].bitcast(I32),
             in_=scales[:, 4 * q : 4 * q + 4, :].rearrange("g r n -> r g n").bitcast(I32),
@@ -76,9 +76,11 @@ def tile_mla_pb_kernel(tc, x_words, x_scales, Wq_words, Wq_scales, out):
         load_codes(nc, w0_first[:], Wq_words[0:1, :, 0 : 2 * N_TILE])
         load_codes(nc, xa_first[:], x_words[0:1, :, 0 : 2 * xh])
         load_plane(nc, w0_plane, Wq_scales[:, :, 0:N_TILE])
-        load_plane(nc, x_planes[0], x_scales[:, :, 0:xh])
+        load_plane(nc, x_planes[0], x_scales[:, :, 0:xh], quadrants=(0, 2))
+        load_plane(nc, x_planes[0][:, 0:1, :], x_scales[0:1, :, 0:xh], quadrants=(1, 3))
         load_codes(nc, w0_rest[:], Wq_words[1:PASSES, :, 0 : 2 * N_TILE])
         load_codes(nc, xa_rest[:], x_words[1:PASSES, :, 0 : 2 * xh])
+        load_plane(nc, x_planes[0][:, 1:PASSES, :], x_scales[1:PASSES, :, 0:xh], quadrants=(1, 3))
         load_codes(nc, xb_codes[:], x_words[:, :, 2 * xh : 4 * xh])
         load_plane(nc, x_planes[1], x_scales[:, :, xh : 2 * xh])
         load_plane(nc, wr_plane, Wq_scales[:, :, N_TILE : 4 * N_TILE])

@@ -242,8 +242,8 @@ def tile_mla_pb_kernel(tc, x_words, x_scales, Wq_words, Wq_scales, out):
 
         t30 = small_groups(banks[30], ((0, 2), (2, 2)))
         t31a = small_groups(banks[31], ((0, 2),))
-        finish(nc.scalar, *t30)
         t31b = small_groups(banks[31], ((2, 1),))
+        finish(nc.scalar, *t30)
         t31c = small_groups(banks[31], ((3, 1),))
         finish(nc.sync, *t31a)
         finish(nc.scalar, *t31b)

@@ -244,7 +244,7 @@ def tile_mla_pb_kernel(tc, x_words, x_scales, Wq_words, Wq_scales, out):
         t31a = small_groups(banks[31], ((0, 2),))
         t31b = small_groups(banks[31], ((2, 1),))
         finish(nc.scalar, *t30)
-        t31c = small_groups(banks[31], ((3, 1),))
         finish(nc.sync, *t31a)
+        t31c = small_groups(banks[31], ((3, 1),))
         finish(nc.scalar, *t31b)
         finish(nc.sync, *t31c)

@@ -243,7 +243,12 @@ def tile_mla_pb_kernel(tc, x_words, x_scales, Wq_words, Wq_scales, out):
         t30 = small_groups(banks[30], ((0, 2), (2, 2)))
         t31a = small_groups(banks[31], ((0, 2),))
         t31b = small_groups(banks[31], ((2, 1),))
-        finish(nc.scalar, *t30)
+        piece30, prod30, res30 = t30
+        for u, queue in ((0, nc.sync), (1, nc.scalar)):
+            rot = res30[:, 2 * u : 2 * u + 2, NOPE:DH].rearrange("p s (f j) -> p s f j", f=2)
+            terms = prod30[:, 2 * u : 2 * u + 2].rearrange("p s f (j e) -> p s f e j", e=2)
+            nc.vector.tensor_tensor(out=rot, in0=terms[:, :, :, 0, :], in1=terms[:, :, :, 1, :], op=ALU.add)
+            store((piece30[0], piece30[1] + 2 * u, 2), res30, 2 * u, queue)
         finish(nc.sync, *t31a)
         t31c = small_groups(banks[31], ((3, 1),))
         finish(nc.scalar, *t31b)

@@ -38,6 +38,14 @@ def load_plane(nc, plane, scales, quadrants=(0, 2, 1, 3)):
         )
 
 
+def load_plane_by_row(nc, plane, scales):
+    for r in range(4):
+        nc.sync.dma_start(
+            out=plane[r : P : 32, :, :].bitcast(I32),
+            in_=scales[:, r : 16 : 4, :].rearrange("g q n -> q g n").bitcast(I32),
+        )
+
+
 def load_codes(nc, codes, words):
     nc.sync.dma_start(out=codes.bitcast(I32), in_=words.rearrange("g p n -> p g n").bitcast(I32))
 
@@ -82,8 +90,8 @@ def tile_mla_pb_kernel(tc, x_words, x_scales, Wq_words, Wq_scales, out):
         load_codes(nc, xa_rest[:], x_words[1:PASSES, :, 0 : 2 * xh])
         load_plane(nc, x_planes[0][:, 1:PASSES, :], x_scales[1:PASSES, :, 0:xh], quadrants=(1, 3))
         load_codes(nc, xb_codes[:], x_words[:, :, 2 * xh : 4 * xh])
-        load_plane(nc, x_planes[1], x_scales[:, :, xh : 2 * xh])
-        load_plane(nc, wr_plane, Wq_scales[:, :, N_TILE : 4 * N_TILE])
+        load_plane_by_row(nc, x_planes[1], x_scales[:, :, xh : 2 * xh])
+        load_plane_by_row(nc, wr_plane, Wq_scales[:, :, N_TILE : 4 * N_TILE])
         load_codes(nc, wr_codes[:], Wq_words[:, :, 2 * N_TILE : 8 * N_TILE])
 
         def x_operand(i, g):

import math
from contextlib import ExitStack

import concourse.mybir as mybir

F32 = mybir.dt.float32
I32 = mybir.dt.int32
BF16 = mybir.dt.bfloat16
U8 = mybir.dt.uint8
FP4X4 = mybir.dt.float4_e2m1fn_x4
ALU = mybir.AluOpType
ACT = mybir.ActivationFunctionType

P = 128
PASSES = 4
TOKENS = 1024
HEADS = 16
DH = 128
NOPE = 32
HALF = 48
SEQ = 512
N_TILE = 512
HB = 4
TOK_TILES = TOKENS // P
POS_TILES = SEQ // P
COL_BLOCKS = HEADS // HB

WARM_UP = 12

FLOPS = 2 * TOKENS * 2048 * 2048


def load_plane(nc, plane, scales, quadrants=(0, 2, 1, 3)):
    for q in quadrants:
        nc.sync.dma_start(
            out=plane[32 * q : 32 * q + 4, :, :].bitcast(I32),
            in_=scales[:, 4 * q : 4 * q + 4, :].rearrange("g r n -> r g n").bitcast(I32),
        )


def load_plane_by_row(nc, plane, scales):
    for r in range(4):
        nc.sync.dma_start(
            out=plane[r : P : 32, :, :].bitcast(I32),
            in_=scales[:, r : 16 : 4, :].rearrange("g q n -> q g n").bitcast(I32),
        )


def load_codes(nc, codes, words):
    nc.sync.dma_start(out=codes.bitcast(I32), in_=words.rearrange("g p n -> p g n").bitcast(I32))


def tile_mla_pb_kernel(tc, x_words, x_scales, Wq_words, Wq_scales, out):
    nc = tc.nc
    with ExitStack() as ctx:
        keep = ctx.enter_context(tc.tile_pool(name="keep", bufs=1))
        work = ctx.enter_context(tc.tile_pool(name="work", bufs=8))
        psum = ctx.enter_context(tc.psum_pool(name="psum", bufs=8))
        ctx.enter_context(tc.manual_schedule())

        xh = TOKENS // 2
        xa_first = keep.tile([P, 1, 2 * xh], U8, name="xa_first", align_bytes=64)
        xa_rest = keep.tile([P, PASSES - 1, 2 * xh], U8, name="xa_rest", align_bytes=64)
        xb_codes = keep.tile([P, PASSES, 2 * xh], U8, name="xb_codes", align_bytes=64)
        x_planes = [keep.tile([P, PASSES, xh], U8, name="x_plane%d" % c, align_bytes=64) for c in range(2)]
        w0_first = keep.tile([P, 1, 2 * N_TILE], U8, name="w0_first", align_bytes=64)
        w0_rest = keep.tile([P, PASSES - 1, 2 * N_TILE], U8, name="w0_rest", align_bytes=64)
        w0_plane = keep.tile([P, PASSES, N_TILE], U8, name="w0_plane", align_bytes=64)
        wr_codes = keep.tile([P, PASSES, 6 * N_TILE], U8, name="wr_codes", align_bytes=64)
        wr_plane = keep.tile([P, PASSES, 3 * N_TILE], U8, name="wr_plane", align_bytes=64)

        zeros = keep.tile([P, N_TILE], BF16, name="zeros")
        nc.gpsimd.memset(zeros[:], 0.0)
        idle = psum.tile([P, N_TILE], F32, name="acc", tag="acc")
        for k in range(WARM_UP):
            nc.tensor.matmul(out=idle[:], lhsT=zeros[:, 0:P], rhs=zeros[:], start=True, stop=True)

        for plane in (w0_plane, x_planes[0], x_planes[1], wr_plane):
            nc.vector.memset(plane[:].bitcast(I32), 0)

        pos = keep.tile([P, POS_TILES], F32, name="pos")
        nc.gpsimd.iota(pos[:], pattern=[[P, POS_TILES]], base=0, channel_multiplier=1, allow_small_or_imprecise_dtypes=True)

        load_codes(nc, w0_first[:], Wq_words[0:1, :, 0 : 2 * N_TILE])
        load_codes(nc, xa_first[:], x_words[0:1, :, 0 : 2 * xh])
        load_plane(nc, w0_plane, Wq_scales[:, :, 0:N_TILE])
        load_plane(nc, x_planes[0], x_scales[:, :, 0:xh], quadrants=(0, 2))
        load_plane(nc, x_planes[0][:, 0:1, :], x_scales[0:1, :, 0:xh], quadrants=(1, 3))
        load_codes(nc, w0_rest[:], Wq_words[1:PASSES, :, 0 : 2 * N_TILE])
        load_codes(nc, xa_rest[:], x_words[1:PASSES, :, 0 : 2 * xh])
        load_plane(nc, x_planes[0][:, 1:PASSES, :], x_scales[1:PASSES, :, 0:xh], quadrants=(1, 3))
        load_codes(nc, xb_codes[:], x_words[:, :, 2 * xh : 4 * xh])
        load_plane_by_row(nc, x_planes[1], x_scales[:, :, xh : 2 * xh])
        load_plane_by_row(nc, wr_plane, Wq_scales[:, :, N_TILE : 4 * N_TILE])
        load_codes(nc, wr_codes[:], Wq_words[:, :, 2 * N_TILE : 8 * N_TILE])

        def x_operand(i, g):
            t0 = (i % 4) * P
            if i >= 4:
                codes = xb_codes[:, g, 2 * t0 : 2 * (t0 + P)]
            elif g == 0:
                codes = xa_first[:, 0, 2 * t0 : 2 * (t0 + P)]
            else:
                codes = xa_rest[:, g - 1, 2 * t0 : 2 * (t0 + P)]
            return codes, x_planes[i // 4][:, g, t0 : t0 + P]

        def w_operand(c0, n, g):
            if c0 >= N_TILE:
                c = c0 - N_TILE
                return wr_codes[:, g, 2 * c : 2 * (c + n)], wr_plane[:, g, c : c + n]
            if g == 0:
                return w0_first[:, 0, 2 * c0 : 2 * (c0 + n)], w0_plane[:, g, c0 : c0 + n]
            return w0_rest[:, g - 1, 2 * c0 : 2 * (c0 + n)], w0_plane[:, g, c0 : c0 + n]

        ratio = 10000.0 ** (-1.0 / HALF)
        theta = keep.tile([P, HALF], F32, name="theta")
        nc.vector.memset(theta[:, 0:1], 1.0)
        warm = keep.tile([P, 1], F32, name="warm")
        nc.scalar.activation(out=warm[:], in_=theta[:, 0:1], func=ACT.Sin)
        width = 1
        while width < HALF:
            n = min(width, HALF - width)
            nc.vector.tensor_scalar(out=theta[:, width : width + n], in0=theta[:, 0:n], scalar1=ratio**width, scalar2=None, op0=ALU.mult)
            width += n
        turns = keep.tile([P, POS_TILES, HALF], F32, name="turns")
        nc.vector.scalar_tensor_tensor(
            out=turns[:],
            in0=theta[:].unsqueeze(1).to_broadcast([P, POS_TILES, HALF]),
            scalar=1.0 / (2.0 * math.pi),
            in1=pos[:].unsqueeze(2).to_broadcast([P, POS_TILES, HALF]),
            op0=ALU.mult,
            op1=ALU.mult,
        )
        whole = keep.tile([P, POS_TILES, HALF], I32, name="whole")
        nc.vector.tensor_copy(out=whole[:], in_=turns[:])
        frac = keep.tile([P, POS_TILES, HALF], F32, name="frac")
        nc.vector.tensor_tensor(out=frac[:], in0=turns[:], in1=whole[:], op=ALU.subtract)
        shifted = keep.tile([P, POS_TILES, 4, HALF], F32, name="shifted")
        frac2 = frac[:].unsqueeze(2).to_broadcast([P, POS_TILES, 2, HALF])
        nc.vector.tensor_scalar(out=shifted[:, :, 0:4:3, :], in0=frac2, scalar1=0.25, scalar2=None, op0=ALU.add)
        nc.vector.tensor_copy(out=shifted[:, :, 1:3, :], in_=frac2)
        wrapped = keep.tile([P, POS_TILES, 4, HALF], F32, name="wrapped")
        flat_s = shifted[:].rearrange("p a s j -> p (a s j)")
        nc.vector.scalar_tensor_tensor(
            out=wrapped[:].rearrange("p a s j -> p (a s j)"), in0=flat_s, scalar=0.5, in1=flat_s, op0=ALU.is_gt, op1=ALU.subtract
        )
        table = keep.tile([P, POS_TILES, 2, 2 * HALF], F32, name="table")
        tslots = table[:].rearrange("p a f (j e) -> p a f e j", e=2)
        nc.scalar.activation(out=tslots[:, :, 0, 0, :], in_=wrapped[:, :, 0, :], func=ACT.Sin, scale=-2.0 * math.pi)
        nc.scalar.activation(out=tslots[:, :, 0, 1, :], in_=wrapped[:, :, 1, :], func=ACT.Sin, scale=2.0 * math.pi)
        nc.scalar.activation(out=tslots[:, :, 1, :, :], in_=wrapped[:, :, 2:4, :], func=ACT.Sin, scale=-2.0 * math.pi)

        def one_pass(acc, piece, g):
            i, h0, nh = piece
            lhsT, lhsT_scale = x_operand(i, g)
            rhs, rhs_scale = w_operand(DH * h0, DH * nh, g)
            nc.tensor.matmul_mx(
                out=acc[:],
                lhsT=lhsT.bitcast(FP4X4),
                lhsT_scale=lhsT_scale,
                rhs=rhs.bitcast(FP4X4),
                rhs_scale=rhs_scale,
                start=(g == 0),
                stop=(g == PASSES - 1),
            )

        def multiply(pieces):
            accs = [psum.tile([P, DH * nh], F32, name="acc", tag="acc") for (i, h0, nh) in pieces]
            for acc, piece in zip(accs, pieces):
                one_pass(acc, piece, 0)
            for acc, piece in zip(accs, pieces):
                for g in range(1, PASSES):
                    one_pass(acc, piece, g)
            return accs

        def products(acc, piece, prod, res, s0):
            i, h0, nh = piece
            heads = acc[:].rearrange("p (h d) -> p h d", h=nh)
            nc.vector.tensor_tensor(
                out=prod[:, s0 : s0 + nh],
                in0=heads[:, :, NOPE:DH].unsqueeze(2).to_broadcast([P, nh, 2, 2 * HALF]),
                in1=table[:, i % POS_TILES].unsqueeze(1).to_broadcast([P, nh, 2, 2 * HALF]),
                op=ALU.mult,
            )
            nc.scalar.copy(out=res[:, s0 : s0 + nh, 0:NOPE], in_=heads[:, :, 0:NOPE])

        def add_terms(engine, prod, res, ns):
            rot = res[:, 0:ns, NOPE:DH].rearrange("p s (f j) -> p s f j", f=2)
            terms = prod[:, 0:ns].rearrange("p s f (j e) -> p s f e j", e=2)
            engine.tensor_tensor(out=rot, in0=terms[:, :, :, 0, :], in1=terms[:, :, :, 1, :], op=ALU.add)

        def store(piece, res, s0, queue=None):
            i, h0, nh = piece
            p0 = (i % POS_TILES) * P
            (queue or nc.sync).dma_start(
                out=out[i // POS_TILES, h0 : h0 + nh, p0 : p0 + P, :].rearrange("h p d -> p h d"),
                in_=res[:, s0 : s0 + nh, :],
            )

        def store_halves(piece, res):
            i, h0, nh = piece
            half = nh // 2
            store((i, h0, half), res, 0, nc.sync)
            store((i, h0 + half, nh - half), res, half, nc.scalar)

        def new_tiles():
            prod = work.tile([P, 2 * HB, 2, 2 * HALF], F32, name="prod", tag="prod")
            res = work.tile([P, 2 * HB, DH], F32, name="res", tag="res", align_bytes=512)
            return prod, res

        banks = [(i, HB * nb, HB) for nb in range(COL_BLOCKS) for i in range(TOK_TILES)]
        queues = (nc.sync, nc.scalar)
        accs = {}
        for piece, acc in zip(banks[0:4], multiply(banks[0:4])):
            accs[piece] = acc
        for k in range(0, 26, 2):
            prod, res = new_tiles()
            for u in range(2):
                piece = banks[k + u]
                if piece not in accs:
                    accs[piece] = multiply([piece])[0]
                products(accs[piece], piece, prod, res, HB * u)
            add_terms(nc.gpsimd, prod, res, 2 * HB)
            for u in range(2):
                store(banks[k + u], res, HB * u, queues[u])
        prod26, res26 = new_tiles()
        products(multiply([banks[26]])[0], banks[26], prod26, res26, 0)
        for k in range(27, 30):
            prod, res = new_tiles()
            products(multiply([banks[k]])[0], banks[k], prod, res, 0)
            if k == 27:
                add_terms(nc.vector, prod26, res26, HB)
                store_halves(banks[26], res26)
            add_terms(nc.gpsimd, prod, res, HB)
            store_halves(banks[k], res)
        def small_groups(bank, cuts):
            i, h0, nh = bank
            prod, res = new_tiles()
            for s0, n in cuts:
                piece = (i, h0 + s0, n)
                products(multiply([piece])[0], piece, prod, res, s0 - cuts[0][0])
            return (i, h0 + cuts[0][0], sum(n for s0, n in cuts)), prod, res

        def finish(queue, piece, prod, res):
            add_terms(nc.vector, prod, res, piece[2])
            if piece[2] > 1:
                store_halves(piece, res)
            else:
                store(piece, res, 0, queue)

        t30 = small_groups(banks[30], ((0, 2), (2, 2)))
        t31a = small_groups(banks[31], ((0, 2),))
        t31b = small_groups(banks[31], ((2, 1),))
        piece30, prod30, res30 = t30
        for u, queue in ((0, nc.sync), (1, nc.scalar)):
            rot = res30[:, 2 * u : 2 * u + 2, NOPE:DH].rearrange("p s (f j) -> p s f j", f=2)
            terms = prod30[:, 2 * u : 2 * u + 2].rearrange("p s f (j e) -> p s f e j", e=2)
            nc.vector.tensor_tensor(out=rot, in0=terms[:, :, :, 0, :], in1=terms[:, :, :, 1, :], op=ALU.add)
            store((piece30[0], piece30[1] + 2 * u, 2), res30, 2 * u, queue)
        finish(nc.sync, *t31a)
        t31c = small_groups(banks[31], ((3, 1),))
        finish(nc.scalar, *t31b)
        finish(nc.sync, *t31c)
